import numpy as np
import ml_dtypes

BF16 = ml_dtypes.bfloat16


def bf(x):
    return np.asarray(x, np.float32).astype(BF16)


def f32(x):
    return np.asarray(x, np.float32)


def f64(x):
    return np.asarray(x).astype(np.float64)


def striped(idx):
    return np.tile(idx.reshape(-1, 16).T, (8, 1))


H, D, M, S, K, N = 256, 256, 512, 4096, 2, 8192


def setup_inputs():
    return {"hidden": bf(np.random.standard_normal((H, S))), "w": bf(np.random.standard_normal((H, M)) / np.sqrt(H)), "b": f32(0.1 * np.random.standard_normal((M, 1))), "offs": striped(np.concatenate([np.random.permutation(S) for _ in range(K)]))}


def reference(hidden, w, b, offs):
    idx = offs[:16].T.reshape(-1)
    proj = f64(w).T @ f64(hidden) + f64(b)
    q, k = proj[:D], proj[D:]
    prod = k[:, idx] * np.tile(q, (1, K))
    return prod.sum(axis=0).reshape(K, S).sum(axis=0, keepdims=True) / np.sqrt(D)

@@ -1,0 +1,133 @@
+import math
+
+import concourse.mybir as mybir
+
+BF16, F32, U16 = mybir.dt.bfloat16, mybir.dt.float32, mybir.dt.uint16
+MULT = mybir.AluOpType.mult
+IDENTITY = mybir.ActivationFunctionType.Identity
+COPY = mybir.ActivationFunctionType.Copy
+
+P = 128
+H = 256
+D = 256
+S = 4096
+ENDS = 2
+BANK = 512
+LOAD = 1024
+ROW = 128
+GROUPS = ((256, 256, 512, 1024, 2048), (2048, 1024, 512, 256, 128, 128))
+WARMUP = 3
+
+FLOPS = 2 * H * (2 * D) * S + 2 * D * ENDS * S
+
+
+def cut(widths, most, first=0):
+    pieces = []
+    for width in widths:
+        step = min(width, most)
+        pieces.extend([(start, step) for start in range(first, first + width, step)])
+        first += width
+    return pieces
+
+
+def tile_customrelation_kernel(tc, hidden, w, b, offs, out):
+    nc = tc.nc
+    with (
+        tc.tile_pool(name="held", bufs=1) as held,
+        tc.tile_pool(name="products", bufs=12) as products,
+        tc.tile_pool(name="roundeds", bufs=4) as roundeds,
+        tc.psum_pool(name="projected", bufs=6) as projected,
+        tc.psum_pool(name="summed", bufs=1) as summed,
+    ):
+        offsets = held.tile([P, ENDS * S // 16], U16, name="offsets")
+        weights = held.tile([P, H // P, 2 * D], BF16, name="weights")
+        tokens = held.tile([P, H // P, S], BF16, name="tokens")
+        biases = [held.tile([P, 1], F32, name=f"bias{block}") for block in range(2 * D // P)]
+        queries = [held.tile([P, S], F32, name=f"queries{c}") for c in range(D // P)]
+        keys = [held.tile([P, S], F32, name=f"keys{c}") for c in range(D // P)]
+
+        w_blocks = w.rearrange("(h p) m -> p h m", p=P)
+
+        def load_block(block):
+            members = slice(block * P, (block + 1) * P)
+            nc.sync.dma_start(weights[:, :, members], w_blocks[:, :, members])
+            nc.sync.dma_start(biases[block][:], b[members, :])
+
+        load_block(D // P)
+        hidden_blocks = hidden.rearrange("(h p) t -> p h t", p=P)
+        for group, width in cut((S,), LOAD):
+            for h in range(H // P):
+                is_first = group == 0 and h == 0
+                is_last = group + width == S and h == H // P - 1
+                for first, step in cut((width,), BANK if is_first or is_last else LOAD, group):
+                    nc.sync.dma_start(tokens[:, h, first : first + step], hidden_blocks[:, h, first : first + step])
+        load_block(0)
+        nc.sync.dma_start(offsets[:], offs)
+        load_block(D // P + 1)
+        load_block(1)
+
+        zeros = held.tile([P, BANK], BF16, name="zeros")
+        nc.gpsimd.memset(zeros[:], 0.0)
+        unused = summed.tile([P, BANK], F32, name="unused")
+        for i in range(WARMUP):
+            nc.tensor.matmul(unused[:], zeros[:, :P], zeros[:], start=True, stop=True)
+
+        marked = S // ROW - 1
+        selector = held.tile([P, marked + P], BF16, name="selector")
+        nc.gpsimd.memset(selector[:], 0.0)
+        nc.gpsimd.memset(selector[:, marked : marked + 1], 1.0 / math.sqrt(D))
+
+        def project(block, pieces, rows, vector_helps):
+            projections = [projected.tile([P, width], F32, name="projection") for first, width in pieces]
+            for h in range(H // P):
+                for (first, width), projection in zip(pieces, projections):
+                    nc.tensor.matmul(
+                        projection[:],
+                        weights[:, h, block * P : (block + 1) * P],
+                        tokens[:, h, first : first + width],
+                        start=(h == 0),
+                        stop=(h == H // P - 1),
+                    )
+            for i, ((first, width), projection) in enumerate(zip(pieces, projections)):
+                if vector_helps and i % 2 == 1:
+                    nc.vector.tensor_scalar_add(rows[:, first : first + width], projection[:], biases[block][:])
+                else:
+                    nc.scalar.activation(
+                        rows[:, first : first + width], projection[:], IDENTITY, bias=biases[block][:]
+                    )
+
+        for group, width in cut((S,), LOAD):
+            project(D // P, cut((width,), BANK, group), keys[0], vector_helps=True)
+        for piece in cut(GROUPS[0], BANK):
+            project(0, [piece], queries[0], vector_helps=False)
+        for block, rows in ((D // P + 1, keys[1]), (1, queries[1])):
+            for piece in cut((S,), BANK):
+                project(block, [piece], rows, vector_helps=False)
+
+        scores = summed.tile([P, ROW], F32, name="scores")
+        for c in range(D // P):
+            for first, width in cut(GROUPS[c], S):
+                for e in range(ENDS):
+                    entry = (e * S + first) // 16
+                    product = products.tile([P, width], F32, name="product")
+                    nc.vector.tensor_tensor(
+                        product[:],
+                        keys[c][:].indirect(offsets[:, entry : entry + width // 16]),
+                        queries[c][:, first : first + width],
+                        MULT,
+                    )
+                    rounded = roundeds.tile([P, width], BF16, name="rounded")
+                    nc.scalar.activation(rounded[:], product[:], COPY)
+                    for token in range(first, first + width, ROW):
+                        r = token // ROW
+                        nc.tensor.matmul(
+                            scores[:],
+                            selector[:, marked - r : marked - r + P],
+                            rounded[:, token - first : token - first + ROW],
+                            start=(c == 0 and e == 0 and token == 0),
+                            stop=(c == D // P - 1 and e == ENDS - 1 and token + ROW == S),
+                        )
+
+        result = held.tile([S // ROW, ROW], F32, name="result")
+        nc.vector.tensor_copy(result[:], scores[: S // ROW, :])
+        nc.sync.dma_start(out.rearrange("o (r n) -> (o r) n", n=ROW), result[:])

@@ -15,7 +15,8 @@ ENDS = 2
 BANK = 512
 LOAD = 1024
 ROW = 128
-GROUPS = ((256, 256, 512, 1024, 2048), (2048, 1024, 512, 256, 128, 128))
+ROUND = 1024
+LOOKUPS = (((256, 256, 512, 1024, 2048), (4096,)), ((4096,), (2048, 1024, 512, 256, 128, 128)))
 WARMUP = 3
 
 FLOPS = 2 * H * (2 * D) * S + 2 * D * ENDS * S
@@ -34,8 +35,6 @@ def tile_customrelation_kernel(tc, hidden, w, b, offs, out):
     nc = tc.nc
     with (
         tc.tile_pool(name="held", bufs=1) as held,
-        tc.tile_pool(name="products", bufs=12) as products,
-        tc.tile_pool(name="roundeds", bufs=4) as roundeds,
         tc.psum_pool(name="projected", bufs=6) as projected,
         tc.psum_pool(name="summed", bufs=1) as summed,
     ):
@@ -44,6 +43,8 @@ def tile_customrelation_kernel(tc, hidden, w, b, offs, out):
         tokens = held.tile([P, H // P, S], BF16, name="tokens")
         biases = [held.tile([P, 1], F32, name=f"bias{block}") for block in range(2 * D // P)]
         queries = [held.tile([P, S], F32, name=f"queries{c}") for c in range(D // P)]
+        products = [[held.tile([P, S], F32, name=f"products{c}{e}") for e in range(ENDS)] for c in range(D // P)]
+        roundeds = [[held.tile([P, S], BF16, name=f"roundeds{c}{e}") for e in range(ENDS)] for c in range(D // P)]
         keys = [held.tile([P, S], F32, name=f"keys{c}") for c in range(D // P)]
 
         w_blocks = w.rearrange("(h p) m -> p h m", p=P)
@@ -63,8 +64,8 @@ def tile_customrelation_kernel(tc, hidden, w, b, offs, out):
                     nc.sync.dma_start(tokens[:, h, first : first + step], hidden_blocks[:, h, first : first + step])
         load_block(0)
         nc.sync.dma_start(offsets[:], offs)
-        load_block(D // P + 1)
         load_block(1)
+        load_block(D // P + 1)
 
         zeros = held.tile([P, BANK], BF16, name="zeros")
         nc.gpsimd.memset(zeros[:], 0.0)
@@ -98,35 +99,35 @@ def tile_customrelation_kernel(tc, hidden, w, b, offs, out):
 
         for group, width in cut((S,), LOAD):
             project(D // P, cut((width,), BANK, group), keys[0], vector_helps=True)
-        for piece in cut(GROUPS[0], BANK):
+        for piece in cut(LOOKUPS[0][0], BANK):
             project(0, [piece], queries[0], vector_helps=False)
-        for block, rows in ((D // P + 1, keys[1]), (1, queries[1])):
+        for block, rows in ((1, queries[1]), (D // P + 1, keys[1])):
             for piece in cut((S,), BANK):
                 project(block, [piece], rows, vector_helps=False)
 
         scores = summed.tile([P, ROW], F32, name="scores")
         for c in range(D // P):
-            for first, width in cut(GROUPS[c], S):
-                for e in range(ENDS):
+            for e in range(ENDS):
+                product, rounded = products[c][e], roundeds[c][e]
+                for first, width in cut(LOOKUPS[c][e], S):
                     entry = (e * S + first) // 16
-                    product = products.tile([P, width], F32, name="product")
                     nc.vector.tensor_tensor(
-                        product[:],
+                        product[:, first : first + width],
                         keys[c][:].indirect(offsets[:, entry : entry + width // 16]),
                         queries[c][:, first : first + width],
                         MULT,
                     )
-                    rounded = roundeds.tile([P, width], BF16, name="rounded")
-                    nc.scalar.activation(rounded[:], product[:], COPY)
-                    for token in range(first, first + width, ROW):
-                        r = token // ROW
-                        nc.tensor.matmul(
-                            scores[:],
-                            selector[:, marked - r : marked - r + P],
-                            rounded[:, token - first : token - first + ROW],
-                            start=(c == 0 and e == 0 and token == 0),
-                            stop=(c == D // P - 1 and e == ENDS - 1 and token + ROW == S),
-                        )
+                    for start, step in cut((width,), ROUND, first):
+                        nc.scalar.activation(rounded[:, start : start + step], product[:, start : start + step], COPY)
+                        for token in range(start, start + step, ROW):
+                            r = token // ROW
+                            nc.tensor.matmul(
+                                scores[:],
+                                selector[:, marked - r : marked - r + P],
+                                rounded[:, token : token + ROW],
+                                start=(c == 0 and e == 0 and token == 0),
+                                stop=(c == D // P - 1 and e == ENDS - 1 and token + ROW == S),
+                            )
 
         result = held.tile([S // ROW, ROW], F32, name="result")
         nc.vector.tensor_copy(result[:], scores[: S // ROW, :])

@@ -14,6 +14,7 @@ S = 4096
 ENDS = 2
 BANK = 512
 LOAD = 1024
+DMA_GRID = 256
 ROW = 128
 ROUND = 1024
 LOOKUPS = (((256, 256, 512, 1024, 2048), (4096,)), ((4096,), (2048, 1024, 512, 256, 128, 128)))
@@ -39,8 +40,8 @@ def tile_customrelation_kernel(tc, hidden, w, b, offs, out):
         tc.psum_pool(name="summed", bufs=1) as summed,
     ):
         offsets = held.tile([P, ENDS * S // 16], U16, name="offsets")
-        weights = held.tile([P, H // P, 2 * D], BF16, name="weights")
-        tokens = held.tile([P, H // P, S], BF16, name="tokens")
+        weights = held.tile([P, H // P, 2 * D], BF16, name="weights", align_bytes=DMA_GRID)
+        tokens = held.tile([P, H // P, S], BF16, name="tokens", align_bytes=DMA_GRID)
         biases = [held.tile([P, 1], F32, name=f"bias{block}") for block in range(2 * D // P)]
         queries = [held.tile([P, S], F32, name=f"queries{c}") for c in range(D // P)]
         products = [[held.tile([P, S], F32, name=f"products{c}{e}") for e in range(ENDS)] for c in range(D // P)]

@@ -17,7 +17,8 @@ LOAD = 1024
 DMA_GRID = 256
 ROW = 128
 ROUND = 1024
-LOOKUPS = (((256, 256, 512, 1024, 2048), (4096,)), ((4096,), (2048, 1024, 512, 256, 128, 128)))
+FIRST = (256, 256, 1024, 2560)
+LAST = (2048, 1024, 512, 256, 128, 128)
 WARMUP = 3
 
 FLOPS = 2 * H * (2 * D) * S + 2 * D * ENDS * S
@@ -26,9 +27,11 @@ FLOPS = 2 * H * (2 * D) * S + 2 * D * ENDS * S
 def cut(widths, most, first=0):
     pieces = []
     for width in widths:
-        step = min(width, most)
-        pieces.extend([(start, step) for start in range(first, first + width, step)])
-        first += width
+        end = first + width
+        while first < end:
+            step = min(end - first, most)
+            pieces.append((first, step))
+            first += step
     return pieces
 
 
@@ -100,35 +103,36 @@ def tile_customrelation_kernel(tc, hidden, w, b, offs, out):
 
         for group, width in cut((S,), LOAD):
             project(D // P, cut((width,), BANK, group), keys[0], vector_helps=True)
-        for piece in cut(LOOKUPS[0][0], BANK):
+        for piece in cut(FIRST, BANK):
             project(0, [piece], queries[0], vector_helps=False)
         for block, rows in ((1, queries[1]), (D // P + 1, keys[1])):
             for piece in cut((S,), BANK):
                 project(block, [piece], rows, vector_helps=False)
 
         scores = summed.tile([P, ROW], F32, name="scores")
-        for c in range(D // P):
-            for e in range(ENDS):
-                product, rounded = products[c][e], roundeds[c][e]
-                for first, width in cut(LOOKUPS[c][e], S):
-                    entry = (e * S + first) // 16
-                    nc.vector.tensor_tensor(
-                        product[:, first : first + width],
-                        keys[c][:].indirect(offsets[:, entry : entry + width // 16]),
-                        queries[c][:, first : first + width],
-                        MULT,
+        lookups = [(0, e, group) for group in cut(FIRST, S) for e in range(ENDS)]
+        lookups.append((1, 0, (0, S)))
+        lookups.extend([(1, 1, group) for group in cut(LAST, S)])
+        for c, e, (first, width) in lookups:
+            entry = (e * S + first) // 16
+            product, rounded = products[c][e], roundeds[c][e]
+            nc.vector.tensor_tensor(
+                product[:, first : first + width],
+                keys[c][:].indirect(offsets[:, entry : entry + width // 16]),
+                queries[c][:, first : first + width],
+                MULT,
+            )
+            for begin, step in cut((width,), ROUND, first):
+                nc.scalar.activation(rounded[:, begin : begin + step], product[:, begin : begin + step], COPY)
+                for token in range(begin, begin + step, ROW):
+                    r = token // ROW
+                    nc.tensor.matmul(
+                        scores[:],
+                        selector[:, marked - r : marked - r + P],
+                        rounded[:, token : token + ROW],
+                        start=(c == 0 and e == 0 and token == 0),
+                        stop=(c == D // P - 1 and e == ENDS - 1 and token + ROW == S),
                     )
-                    for start, step in cut((width,), ROUND, first):
-                        nc.scalar.activation(rounded[:, start : start + step], product[:, start : start + step], COPY)
-                        for token in range(start, start + step, ROW):
-                            r = token // ROW
-                            nc.tensor.matmul(
-                                scores[:],
-                                selector[:, marked - r : marked - r + P],
-                                rounded[:, token : token + ROW],
-                                start=(c == 0 and e == 0 and token == 0),
-                                stop=(c == D // P - 1 and e == ENDS - 1 and token + ROW == S),
-                            )
 
         result = held.tile([S // ROW, ROW], F32, name="result")
         nc.vector.tensor_copy(result[:], scores[: S // ROW, :])

@@ -93,8 +93,8 @@ def tile_customrelation_kernel(tc, hidden, w, b, offs, out):
                         start=(h == 0),
                         stop=(h == H // P - 1),
                     )
-            for i, ((first, width), projection) in enumerate(zip(pieces, projections)):
-                if vector_helps and i % 2 == 1:
+            for (first, width), projection in zip(pieces, projections):
+                if vector_helps and first // BANK % 2 == 1:
                     nc.vector.tensor_scalar_add(rows[:, first : first + width], projection[:], biases[block][:])
                 else:
                     nc.scalar.activation(
@@ -102,8 +102,9 @@ def tile_customrelation_kernel(tc, hidden, w, b, offs, out):
                     )
 
         for group, width in cut((S,), LOAD):
-            project(D // P, cut((width,), BANK, group), keys[0], vector_helps=True)
-        for piece in cut(FIRST, BANK):
+            widths = (width - BANK, BANK // 2, BANK // 2) if group + width == S else (width,)
+            project(D // P, cut(widths, BANK, group), keys[0], vector_helps=True)
+        for piece in cut((P, P) + FIRST[1:], BANK):
             project(0, [piece], queries[0], vector_helps=False)
         for block, rows in ((1, queries[1]), (D // P + 1, keys[1])):
             for piece in cut((S,), BANK):
@@ -111,7 +112,7 @@ def tile_customrelation_kernel(tc, hidden, w, b, offs, out):
 
         scores = summed.tile([P, ROW], F32, name="scores")
         lookups = [(0, e, group) for group in cut(FIRST, S) for e in range(ENDS)]
-        lookups.append((1, 0, (0, S)))
+        lookups.extend([(1, 0, group) for group in cut((S,), S // 2)])
         lookups.extend([(1, 1, group) for group in cut(LAST, S)])
         for c, e, (first, width) in lookups:
             entry = (e * S + first) // 16

@@ -19,7 +19,7 @@ ROW = 128
 ROUND = 1024
 FIRST = (256, 256, 1024, 2560)
 LAST = (2048, 1024, 512, 256, 128, 128)
-WARMUP = 3
+WARMUP = 12
 
 FLOPS = 2 * H * (2 * D) * S + 2 * D * ENDS * S
 
@@ -71,11 +71,11 @@ def tile_customrelation_kernel(tc, hidden, w, b, offs, out):
         load_block(1)
         load_block(D // P + 1)
 
-        zeros = held.tile([P, BANK], BF16, name="zeros")
+        zeros = held.tile([P, P], BF16, name="zeros")
         nc.gpsimd.memset(zeros[:], 0.0)
-        unused = summed.tile([P, BANK], F32, name="unused")
+        unused = summed.tile([P, P], F32, name="unused")
         for i in range(WARMUP):
-            nc.tensor.matmul(unused[:], zeros[:, :P], zeros[:], start=True, stop=True)
+            nc.tensor.matmul(unused[:], zeros[:], zeros[:], start=True, stop=True)
 
         marked = S // ROW - 1
         selector = held.tile([P, marked + P], BF16, name="selector")

@@ -13,7 +13,7 @@ D = 256
 S = 4096
 ENDS = 2
 BANK = 512
-LOAD = 1024
+LOADS = (1024, 1024, 1024, 512, 512)
 DMA_GRID = 256
 ROW = 128
 ROUND = 1024
@@ -60,11 +60,10 @@ def tile_customrelation_kernel(tc, hidden, w, b, offs, out):
 
         load_block(D // P)
         hidden_blocks = hidden.rearrange("(h p) t -> p h t", p=P)
-        for group, width in cut((S,), LOAD):
+        for group, width in cut(LOADS, S):
             for h in range(H // P):
                 is_first = group == 0 and h == 0
-                is_last = group + width == S and h == H // P - 1
-                for first, step in cut((width,), BANK if is_first or is_last else LOAD, group):
+                for first, step in cut((width,), BANK if is_first else width, group):
                     nc.sync.dma_start(tokens[:, h, first : first + step], hidden_blocks[:, h, first : first + step])
         load_block(0)
         nc.sync.dma_start(offsets[:], offs)
@@ -101,9 +100,9 @@ def tile_customrelation_kernel(tc, hidden, w, b, offs, out):
                         rows[:, first : first + width], projection[:], IDENTITY, bias=biases[block][:]
                     )
 
-        for group, width in cut((S,), LOAD):
-            widths = (width - BANK, BANK // 2, BANK // 2) if group + width == S else (width,)
-            project(D // P, cut(widths, BANK, group), keys[0], vector_helps=True)
+        for group, width in cut(LOADS, S):
+            is_last = group + width == S
+            project(D // P, cut((width,), BANK // 2 if is_last else BANK, group), keys[0], vector_helps=True)
         for piece in cut((P, P) + FIRST[1:], BANK):
             project(0, [piece], queries[0], vector_helps=False)
         for block, rows in ((1, queries[1]), (D // P + 1, keys[1])):
@@ -124,7 +123,10 @@ def tile_customrelation_kernel(tc, hidden, w, b, offs, out):
                 MULT,
             )
             for begin, step in cut((width,), ROUND, first):
-                nc.scalar.activation(rounded[:, begin : begin + step], product[:, begin : begin + step], COPY)
+                if c == D // P - 1 and e == ENDS - 1 and begin + step == S:
+                    nc.vector.tensor_copy(rounded[:, begin : begin + step], product[:, begin : begin + step])
+                else:
+                    nc.scalar.activation(rounded[:, begin : begin + step], product[:, begin : begin + step], COPY)
                 for token in range(begin, begin + step, ROW):
                     r = token // ROW
                     nc.tensor.matmul(

@@ -58,13 +58,16 @@ def tile_customrelation_kernel(tc, hidden, w, b, offs, out):
             nc.sync.dma_start(weights[:, :, members], w_blocks[:, :, members])
             nc.sync.dma_start(biases[block][:], b[members, :])
 
-        load_block(D // P)
         hidden_blocks = hidden.rearrange("(h p) t -> p h t", p=P)
+        key_columns = slice(D, D + P)
         for group, width in cut(LOADS, S):
             for h in range(H // P):
-                is_first = group == 0 and h == 0
-                for first, step in cut((width,), BANK if is_first else width, group):
+                if group == 0:
+                    nc.sync.dma_start(weights[:, h, key_columns], w_blocks[:, h, key_columns])
+                for first, step in cut((width,), BANK if group == 0 and h == 0 else width, group):
                     nc.sync.dma_start(tokens[:, h, first : first + step], hidden_blocks[:, h, first : first + step])
+            if group == 0:
+                nc.sync.dma_start(biases[D // P][:], b[key_columns, :])
         load_block(0)
         nc.sync.dma_start(offsets[:], offs)
         load_block(1)
@@ -75,6 +78,8 @@ def tile_customrelation_kernel(tc, hidden, w, b, offs, out):
         unused = summed.tile([P, P], F32, name="unused")
         for i in range(WARMUP):
             nc.tensor.matmul(unused[:], zeros[:], zeros[:], start=True, stop=True)
+
+        nc.scalar.activation(held.tile([P, 1], F32, name="unused_column")[:], zeros[:, :1], COPY)
 
         marked = S // ROW - 1
         selector = held.tile([P, marked + P], BF16, name="selector")

@@ -17,7 +17,7 @@ LOADS = (1024, 1024, 1024, 512, 512)
 DMA_GRID = 256
 ROW = 128
 ROUND = 1024
-FIRST = (256, 256, 1024, 2560)
+REACHES = (256, 256, 512, 1024, 2048, 4096, 4096)
 LAST = (2048, 1024, 512, 256, 128, 128)
 WARMUP = 12
 
@@ -42,7 +42,7 @@ def tile_customrelation_kernel(tc, hidden, w, b, offs, out):
         tc.psum_pool(name="projected", bufs=6) as projected,
         tc.psum_pool(name="summed", bufs=1) as summed,
     ):
-        offsets = held.tile([P, ENDS * S // 16], U16, name="offsets")
+        offsets = held.tile([P, ENDS * S // 16], U16, name="offsets", align_bytes=DMA_GRID)
         weights = held.tile([P, H // P, 2 * D], BF16, name="weights", align_bytes=DMA_GRID)
         tokens = held.tile([P, H // P, S], BF16, name="tokens", align_bytes=DMA_GRID)
         biases = [held.tile([P, 1], F32, name=f"bias{block}") for block in range(2 * D // P)]
@@ -108,15 +108,20 @@ def tile_customrelation_kernel(tc, hidden, w, b, offs, out):
         for group, width in cut(LOADS, S):
             is_last = group + width == S
             project(D // P, cut((width,), BANK // 2 if is_last else BANK, group), keys[0], vector_helps=True)
-        for piece in cut((P, P) + FIRST[1:], BANK):
+        for piece in cut((P, P, 2 * P, S - 4 * P), BANK):
             project(0, [piece], queries[0], vector_helps=False)
         for block, rows in ((1, queries[1]), (D // P + 1, keys[1])):
             for piece in cut((S,), BANK):
                 project(block, [piece], rows, vector_helps=False)
 
         scores = summed.tile([P, ROW], F32, name="scores")
-        lookups = [(0, e, group) for group in cut(FIRST, S) for e in range(ENDS)]
-        lookups.extend([(1, 0, group) for group in cut((S,), S // 2)])
+        lookups = []
+        done = [0] * ENDS
+        for i, reach in enumerate(REACHES):
+            e = i % ENDS
+            lookups.append((0, e, (done[e], reach - done[e])))
+            done[e] = reach
+        lookups.append((1, 0, (0, S)))
         lookups.extend([(1, 1, group) for group in cut(LAST, S)])
         for c, e, (first, width) in lookups:
             entry = (e * S + first) // 16

import math

import concourse.mybir as mybir

BF16, F32, U16 = mybir.dt.bfloat16, mybir.dt.float32, mybir.dt.uint16
MULT = mybir.AluOpType.mult
IDENTITY = mybir.ActivationFunctionType.Identity
COPY = mybir.ActivationFunctionType.Copy

P = 128
H = 256
D = 256
S = 4096
ENDS = 2
BANK = 512
LOADS = (1024, 1024, 1024, 512, 512)
DMA_GRID = 256
ROW = 128
ROUND = 1024
REACHES = (256, 256, 512, 1024, 2048, 4096, 4096)
LAST = (2048, 1024, 512, 256, 128, 128)
WARMUP = 12

FLOPS = 2 * H * (2 * D) * S + 2 * D * ENDS * S


def cut(widths, most, first=0):
    pieces = []
    for width in widths:
        end = first + width
        while first < end:
            step = min(end - first, most)
            pieces.append((first, step))
            first += step
    return pieces


def tile_customrelation_kernel(tc, hidden, w, b, offs, out):
    nc = tc.nc
    with (
        tc.tile_pool(name="held", bufs=1) as held,
        tc.psum_pool(name="projected", bufs=6) as projected,
        tc.psum_pool(name="summed", bufs=1) as summed,
    ):
        offsets = held.tile([P, ENDS * S // 16], U16, name="offsets", align_bytes=DMA_GRID)
        weights = held.tile([P, H // P, 2 * D], BF16, name="weights", align_bytes=DMA_GRID)
        tokens = held.tile([P, H // P, S], BF16, name="tokens", align_bytes=DMA_GRID)
        biases = [held.tile([P, 1], F32, name=f"bias{block}") for block in range(2 * D // P)]
        queries = [held.tile([P, S], F32, name=f"queries{c}") for c in range(D // P)]
        products = [[held.tile([P, S], F32, name=f"products{c}{e}") for e in range(ENDS)] for c in range(D // P)]
        roundeds = [[held.tile([P, S], BF16, name=f"roundeds{c}{e}") for e in range(ENDS)] for c in range(D // P)]
        keys = [held.tile([P, S], F32, name=f"keys{c}") for c in range(D // P)]

        w_blocks = w.rearrange("(h p) m -> p h m", p=P)

        def load_block(block):
            members = slice(block * P, (block + 1) * P)
            nc.sync.dma_start(weights[:, :, members], w_blocks[:, :, members])
            nc.sync.dma_start(biases[block][:], b[members, :])

        hidden_blocks = hidden.rearrange("(h p) t -> p h t", p=P)
        key_columns = slice(D, D + P)
        for group, width in cut(LOADS, S):
            for h in range(H // P):
                if group == 0:
                    nc.sync.dma_start(weights[:, h, key_columns], w_blocks[:, h, key_columns])
                for first, step in cut((width,), BANK if group == 0 and h == 0 else width, group):
                    nc.sync.dma_start(tokens[:, h, first : first + step], hidden_blocks[:, h, first : first + step])
            if group == 0:
                nc.sync.dma_start(biases[D // P][:], b[key_columns, :])
        load_block(0)
        nc.sync.dma_start(offsets[:], offs)
        load_block(1)
        load_block(D // P + 1)

        zeros = held.tile([P, P], BF16, name="zeros")
        nc.gpsimd.memset(zeros[:], 0.0)
        unused = summed.tile([P, P], F32, name="unused")
        for i in range(WARMUP):
            nc.tensor.matmul(unused[:], zeros[:], zeros[:], start=True, stop=True)

        nc.scalar.activation(held.tile([P, 1], F32, name="unused_column")[:], zeros[:, :1], COPY)

        marked = S // ROW - 1
        selector = held.tile([P, marked + P], BF16, name="selector")
        nc.gpsimd.memset(selector[:], 0.0)
        nc.gpsimd.memset(selector[:, marked : marked + 1], 1.0 / math.sqrt(D))

        def project(block, pieces, rows, vector_helps):
            projections = [projected.tile([P, width], F32, name="projection") for first, width in pieces]
            for h in range(H // P):
                for (first, width), projection in zip(pieces, projections):
                    nc.tensor.matmul(
                        projection[:],
                        weights[:, h, block * P : (block + 1) * P],
                        tokens[:, h, first : first + width],
                        start=(h == 0),
                        stop=(h == H // P - 1),
                    )
            for (first, width), projection in zip(pieces, projections):
                if vector_helps and first // BANK % 2 == 1:
                    nc.vector.tensor_scalar_add(rows[:, first : first + width], projection[:], biases[block][:])
                else:
                    nc.scalar.activation(
                        rows[:, first : first + width], projection[:], IDENTITY, bias=biases[block][:]
                    )

        for group, width in cut(LOADS, S):
            is_last = group + width == S
            project(D // P, cut((width,), BANK // 2 if is_last else BANK, group), keys[0], vector_helps=True)
        for piece in cut((P, P, 2 * P, S - 4 * P), BANK):
            project(0, [piece], queries[0], vector_helps=False)
        for block, rows in ((1, queries[1]), (D // P + 1, keys[1])):
            for piece in cut((S,), BANK):
                project(block, [piece], rows, vector_helps=False)

        scores = summed.tile([P, ROW], F32, name="scores")
        lookups = []
        done = [0] * ENDS
        for i, reach in enumerate(REACHES):
            e = i % ENDS
            lookups.append((0, e, (done[e], reach - done[e])))
            done[e] = reach
        lookups.append((1, 0, (0, S)))
        lookups.extend([(1, 1, group) for group in cut(LAST, S)])
        for c, e, (first, width) in lookups:
            entry = (e * S + first) // 16
            product, rounded = products[c][e], roundeds[c][e]
            nc.vector.tensor_tensor(
                product[:, first : first + width],
                keys[c][:].indirect(offsets[:, entry : entry + width // 16]),
                queries[c][:, first : first + width],
                MULT,
            )
            for begin, step in cut((width,), ROUND, first):
                if c == D // P - 1 and e == ENDS - 1 and begin + step == S:
                    nc.vector.tensor_copy(rounded[:, begin : begin + step], product[:, begin : begin + step])
                else:
                    nc.scalar.activation(rounded[:, begin : begin + step], product[:, begin : begin + step], COPY)
                for token in range(begin, begin + step, ROW):
                    r = token // ROW
                    nc.tensor.matmul(
                        scores[:],
                        selector[:, marked - r : marked - r + P],
                        rounded[:, token : token + ROW],
                        start=(c == 0 and e == 0 and token == 0),
                        stop=(c == D // P - 1 and e == ENDS - 1 and token + ROW == S),
                    )

        result = held.tile([S // ROW, ROW], F32, name="result")
        nc.vector.tensor_copy(result[:], scores[: S // ROW, :])
        nc.sync.dma_start(out.rearrange("o (r n) -> (o r) n", n=ROW), result[:])
